import numpy as np
import ml_dtypes


def mxq(x, axis, fmt="e4m3"):
    dtype, down = {"e4m3": (ml_dtypes.float8_e4m3fn, 7), "e5m2": (ml_dtypes.float8_e5m2, 14)}[fmt]
    v = np.moveaxis(np.asarray(x, np.float32).astype(ml_dtypes.bfloat16).astype(np.float64), axis, -1)
    blocks = v.reshape(v.shape[:-1] + (-1, 32))
    amax = np.abs(blocks).max(-1, keepdims=True)
    byte = np.maximum(np.where(amax > 0, np.frexp(amax)[1] - 1 + 127, 0) - down, 1)
    scale = np.exp2(byte - 127.0)
    codes = (blocks / scale).astype(np.float32).astype(dtype).astype(np.float64)
    return np.moveaxis((codes * scale).reshape(v.shape), -1, axis)


WIDE = False


def mx_kscale(k):
    if not WIDE:
        return np.ones(k)
    levels = np.array([30, -30])
    if k % 512:
        return np.exp2(np.random.permutation(np.resize(levels, k // 32))).repeat(32)
    a = np.empty((k // 512, 16))
    for p in range(k // 512):
        a[p, :8] = np.random.permutation(np.resize(levels, 8))
        for g in range(8):
            far = levels[np.abs(levels - a[p, g]) >= 10]
            a[p, g + 8] = far[np.random.randint(len(far))]
    return np.exp2(a.ravel()).repeat(32)


BF16 = ml_dtypes.bfloat16


def bf(x):
    return np.asarray(x, np.float32).astype(BF16)


def f64(x):
    return np.asarray(x).astype(np.float64)


B, I, H = 1024, 1024, 1024
G = 2 * H
EPS = 1e-5


def ln(v):
    mu = v.mean(-1, keepdims=True)
    var = np.square(v - mu).mean(-1, keepdims=True)
    return (v - mu) / np.sqrt(var + EPS)


def sigmoid(v):
    return 1.0 / (1.0 + np.exp(-v))


def setup_inputs():
    s, t = mx_kscale(I), mx_kscale(H)
    return {"x": bf(np.random.standard_normal((B, I)) * s),
            "h": bf(np.random.standard_normal((B, H)) * t),
            "W_irz": bf(np.random.standard_normal((G, I)) / np.sqrt(I) / s),
            "b_irz": bf(np.random.standard_normal(G) * 0.5),
            "W_hrz": bf(np.random.standard_normal((G, H)) / np.sqrt(H) / t),
            "b_hrz": bf(np.random.standard_normal(G) * 0.5)}


def reference(x, h, W_irz, b_irz, W_hrz, b_hrz):
    i_rz = ln((mxq(f64(x), 1, "e5m2") @ mxq(f64(W_irz), 1, "e5m2").T) + f64(b_irz))
    h_rz = ln((mxq(f64(h), 1, "e5m2") @ mxq(f64(W_hrz), 1, "e5m2").T) + f64(b_hrz))
    return sigmoid(i_rz + h_rz)

@@ -1,0 +1,300 @@
+from contextlib import ExitStack
+
+import concourse.mybir as mybir
+from concourse.masks import make_identity
+
+F32 = mybir.dt.float32
+BF16 = mybir.dt.bfloat16
+I32 = mybir.dt.int32
+U32 = mybir.dt.uint32
+U8 = mybir.dt.uint8
+E5X4 = mybir.dt.float8_e5m2_x4
+ALU = mybir.AluOpType
+ACT = mybir.ActivationFunctionType
+
+ROWS, K, GATES = 1024, 1024, 2048
+FLOPS = 2 * 2 * ROWS * K * GATES
+
+P = 128
+NT = 512
+PASSES = K // (4 * P)
+RT = ROWS // P
+CH = GATES // NT
+EPS = 1e-5
+W_COPY = ("S", "S", "V", "S")
+XH_COPY = ("S", "S")
+HALF = GATES // 2
+
+
+def tile_layernormgrucell_pa_kernel(tc, x, h, W_irz, b_irz, W_hrz, b_hrz, out):
+    nc = tc.nc
+    with ExitStack() as ctx:
+        const = ctx.enter_context(tc.tile_pool(name="const", bufs=1))
+        wraw = ctx.enter_context(tc.tile_pool(name="wraw", bufs=8))
+        grp = ctx.enter_context(tc.tile_pool(name="grp", bufs=3))
+        keep = ctx.enter_context(tc.tile_pool(name="keep", bufs=1))
+        acts = ctx.enter_context(tc.tile_pool(name="acts", bufs=3))
+        ypool = ctx.enter_context(tc.tile_pool(name="ypool", bufs=3))
+        small = ctx.enter_context(tc.tile_pool(name="small", bufs=3))
+        psum = ctx.enter_context(tc.psum_pool(name="psum", bufs=8))
+        ctx.enter_context(tc.manual_schedule())
+
+        warm = const.tile([P, 1], F32, name="warm")
+        nc.vector.memset(warm[:], 0.0)
+        warm2 = const.tile([P, 1], F32, name="warm2")
+        nc.scalar.activation(out=warm2[:], in_=warm[:], func=ACT.Sigmoid)
+        ident = const.tile([P, P], F32, name="ident")
+        make_identity(nc, ident[:])
+        brow = const.tile([P, 2 * GATES], BF16, name="brow")
+        nc.vector.memset(brow[:].bitcast(I32), 0)
+        ones = const.tile([P, P], BF16, name="ones")
+        nc.vector.memset(ones[:], 1.0)
+        sums = const.tile([P, RT * 2 * CH], F32, name="sums")
+        tot = const.tile([P, RT * 2], F32, name="tot")
+        qq = const.tile([P, RT * 2], F32, name="qq")
+        neghalf = const.tile([P, 2], F32, name="neghalf")
+        nc.vector.memset(neghalf[:], -0.5)
+        bias = const.tile([P, 2 * GATES], BF16, name="bias")
+
+        weights = (W_irz, W_hrz)
+        rows_in = (x, h)
+        wr = {}
+        ar = {}
+
+        def load_w(s, c):
+            for hf in range(2):
+                t = wraw.tile([P, 2, K], BF16, name="wr", tag="wr")
+                r0 = c * NT + hf * 2 * P
+                nc.sync.dma_start(
+                    out=t[:], in_=weights[s][r0 : r0 + 2 * P, :].rearrange("(j p) k -> p j k", p=P)
+                )
+                wr[(s, c, hf)] = t
+
+        def load_a(s, m):
+            t = const.tile([P, K], BF16, name="ar%d_%d" % (s, m))
+            nc.sync.dma_start(out=t[:], in_=rows_in[s][m * P : (m + 1) * P, :])
+            ar[(s, m)] = t
+
+        load_a(0, 0)
+        load_a(1, 0)
+        load_w(0, 0)
+        nc.sync.dma_start(out=brow[0:1, 0:GATES], in_=b_irz.rearrange("(o n) -> o n", o=1))
+        nc.sync.dma_start(out=brow[0:1, GATES : 2 * GATES], in_=b_hrz.rearrange("(o n) -> o n", o=1))
+        for c in range(1, CH):
+            load_w(0, c)
+        for c in range(CH):
+            load_w(1, c)
+        for m in range(1, RT):
+            load_a(0, m)
+            load_a(1, m)
+
+        def transpose_rows(raw2d):
+            words = raw2d.bitcast(F32)
+            bank = psum.tile([P, NT], F32, name="tbank", tag="bank")
+            for g in range(PASSES):
+                for u in range(2):
+                    q = 2 * g + u
+                    nc.tensor.transpose(
+                        bank[:, q * P : (q + 1) * P],
+                        words[:, 256 * g + u : 256 * (g + 1) : 2],
+                        ident[:],
+                    )
+            return bank
+
+        def copy_out(eng, dst_words, bank):
+            src = bank[:].rearrange("p (g u r) -> p g r u", g=PASSES, u=2)
+            if eng == "S":
+                nc.scalar.copy(out=dst_words, in_=src)
+            else:
+                nc.vector.tensor_copy(out=dst_words, in_=src)
+
+        gw = {}
+        cw = {}
+        sw = {}
+
+        def turn_w(s, c):
+            grouped = grp.tile([P, PASSES, NT, 4], BF16, name="gw", tag="gw", align_bytes=64)
+            gwords = grouped[:].bitcast(F32)
+            banks = [transpose_rows(wr[(s, c, j // 2)][:, j % 2, :]) for j in range(4)]
+            for j in range(4):
+                copy_out(W_COPY[j], gwords[:, :, j * P : (j + 1) * P, :], banks[j])
+            gw[(s, c)] = grouped
+
+        def quant_w(s, c):
+            codes = keep.tile([P, PASSES, NT], U32, name="cw%d_%d" % (s, c), align_bytes=64)
+            scales = keep.tile([P, PASSES, NT], U8, name="sw%d_%d" % (s, c), align_bytes=64)
+            nc.vector.quantize_mx(
+                out=codes[:].rearrange("p g n -> p (g n)").bitcast(E5X4),
+                scales=scales[:].rearrange("p g n -> p (g n)"),
+                in_=gw[(s, c)][:].rearrange("p g n t -> p (g n t)"),
+            )
+            cw[(s, c)] = codes
+            sw[(s, c)] = scales
+
+        ga = {}
+        ca = {}
+        sa = {}
+
+        def turn_a(m):
+            grouped = grp.tile([P, 2, PASSES, P, 4], BF16, name="ga", tag="ga", align_bytes=64)
+            gwords = grouped[:].bitcast(F32)
+            banks = [transpose_rows(ar[(s, m)][:]) for s in range(2)]
+            for s in range(2):
+                copy_out(XH_COPY[s], gwords[:, s, :, :, :], banks[s])
+            ga[m] = grouped
+
+        def quant_a(m):
+            codes = acts.tile([P, 2, PASSES, P], U32, name="ca", tag="ca", align_bytes=64)
+            scales = acts.tile([P, 2, PASSES, P], U8, name="sa", tag="sa", align_bytes=64)
+            nc.vector.quantize_mx(
+                out=codes[:].rearrange("p s g n -> p (s g n)").bitcast(E5X4),
+                scales=scales[:].rearrange("p s g n -> p (s g n)"),
+                in_=ga[m][:].rearrange("p s g n t -> p (s g n t)"),
+            )
+            ca[m] = codes
+            sa[m] = scales
+
+        def spread_bias(jb):
+            pb = psum.tile([P, NT], F32, name="pb", tag="bank")
+            cols = slice(jb * NT, (jb + 1) * NT)
+            nc.tensor.matmul(out=pb[:], lhsT=ones[:], rhs=brow[:, cols], start=True, stop=True)
+            if jb % 2 == 0:
+                nc.vector.tensor_copy(out=bias[:, cols], in_=pb[:])
+            else:
+                nc.scalar.copy(out=bias[:, cols], in_=pb[:])
+
+        accs = {}
+        ys = {}
+
+        def multiply(m, s):
+            for c in range(CH):
+                acc = psum.tile([P, NT], F32, name="acc", tag="bank")
+                for g in range(PASSES):
+                    nc.tensor.matmul_mx(
+                        out=acc[:],
+                        lhsT=ca[m][:, s, g, :].bitcast(E5X4),
+                        lhsT_scale=sa[m][:, s, g, :],
+                        rhs=cw[(s, c)][:, g, :].bitcast(E5X4),
+                        rhs_scale=sw[(s, c)][:, g, :],
+                        start=(g == 0),
+                        stop=(g == PASSES - 1),
+                    )
+                accs[(m, s, c)] = acc
+
+        def empty(m, s):
+            y = ypool.tile([P, GATES], F32, name="y%d" % s, tag="y%d" % s)
+            ys[(m, s)] = y
+            i = m * 2 + s
+            for c in range(CH):
+                nc.vector.scalar_tensor_tensor(
+                    out=y[:, c * NT : (c + 1) * NT],
+                    in0=accs[(m, s, c)][:],
+                    scalar=1.0,
+                    in1=bias[:, s * GATES + c * NT : s * GATES + (c + 1) * NT],
+                    op0=ALU.mult,
+                    op1=ALU.add,
+                    accum_out=sums[:, i * CH + c : i * CH + c + 1],
+                )
+
+        def row_sum(m, s):
+            i = m * 2 + s
+            nc.vector.tensor_reduce(
+                out=tot[:, i : i + 1], in_=sums[:, i * CH : (i + 1) * CH], axis=mybir.AxisListType.X, op=ALU.add
+            )
+
+        def square(m, s):
+            i = m * 2 + s
+            junk = small.tile([P, GATES], BF16, name="junk", tag="junk", bufs=2)
+            nc.scalar.activation(
+                out=junk[:],
+                in_=ys[(m, s)][:],
+                func=ACT.Square,
+                bias=tot[:, i : i + 1],
+                scale=-2048.0,
+                accum_out=qq[:, i : i + 1],
+            )
+
+        fac = {}
+
+        def factors(m):
+            i = m * 2
+            vv = small.tile([P, 2], F32, name="vv", tag="vv")
+            nc.gpsimd.tensor_scalar(
+                out=vv[:], in0=qq[:, i : i + 2], scalar1=2.0 ** -33, scalar2=EPS, op0=ALU.mult, op1=ALU.add
+            )
+            rr = small.tile([P, 2], F32, name="rr", tag="rr")
+            nc.gpsimd.tensor_tensor(out=rr[:], in0=vv[:], in1=neghalf[:], op=ALU.pow)
+            rho = small.tile([P, 1], F32, name="rho", tag="rho")
+            nc.gpsimd.tensor_scalar(
+                out=rho[:], in0=vv[:, 0:1], scalar1=rr[:, 0:1], scalar2=rr[:, 1:2], op0=ALU.mult, op1=ALU.mult
+            )
+            kp = small.tile([P, 1], F32, name="kp", tag="kp")
+            nc.gpsimd.tensor_scalar(
+                out=kp[:], in0=tot[:, i + 1 : i + 2], scalar1=rho[:, 0:1], scalar2=tot[:, i : i + 1], op0=ALU.mult, op1=ALU.add
+            )
+            cc = small.tile([P, 1], F32, name="cc", tag="cc")
+            nc.gpsimd.tensor_scalar(
+                out=cc[:], in0=kp[:], scalar1=rr[:, 0:1], scalar2=-(2.0 ** -11), op0=ALU.mult, op1=ALU.mult
+            )
+            fac[m] = (rr, rho, cc)
+
+        def combine(m, hf):
+            y1 = ys[(m, 0)]
+            y2 = ys[(m, 1)]
+            rho = fac[m][1]
+            cols = slice(hf * HALF, (hf + 1) * HALF)
+            nc.vector.scalar_tensor_tensor(
+                out=y1[:, cols], in0=y2[:, cols], scalar=rho[:, 0:1], in1=y1[:, cols], op0=ALU.mult, op1=ALU.add
+            )
+
+        def squash(m):
+            y1 = ys[(m, 0)]
+            rr = fac[m][0]
+            cc = fac[m][2]
+            for hf in range(2):
+                cols = slice(hf * HALF, (hf + 1) * HALF)
+                nc.scalar.activation(
+                    out=y1[:, cols], in_=y1[:, cols], func=ACT.Sigmoid, bias=cc[:, 0:1], scale=rr[:, 0:1]
+                )
+                nc.sync.dma_start(out=out[m * P : (m + 1) * P, cols], in_=y1[:, cols])
+
+        chunks = [(s, c) for s in range(2) for c in range(CH)]
+        turn_a(0)
+        for q in range(2 * CH):
+            turn_w(chunks[q][0], chunks[q][1])
+            if q == 0:
+                quant_a(0)
+            else:
+                quant_w(chunks[q - 1][0], chunks[q - 1][1])
+            if 2 <= q < 6:
+                spread_bias(2 * (q - 2))
+                spread_bias(2 * (q - 2) + 1)
+        turn_a(1)
+        multiply(0, 0)
+        quant_w(1, CH - 1)
+        for i in range(RT + 2):
+            if i >= 2:
+                squash(i - 2)
+            if 1 <= i <= RT:
+                factors(i - 1)
+            if i < RT:
+                empty(i, 0)
+                if i + 1 < RT:
+                    quant_a(i + 1)
+                row_sum(i, 0)
+                square(i, 0)
+                multiply(i, 1)
+                if i + 2 < RT:
+                    turn_a(i + 2)
+                empty(i, 1)
+                if i >= 1:
+                    combine(i - 1, 0)
+                row_sum(i, 1)
+                square(i, 1)
+                if i + 1 < RT:
+                    multiply(i + 1, 0)
+                if i >= 1:
+                    combine(i - 1, 1)
+            if i == RT:
+                combine(i - 1, 0)
+                combine(i - 1, 1)

@@ -5,7 +5,6 @@ from concourse.masks import make_identity
 
 F32 = mybir.dt.float32
 BF16 = mybir.dt.bfloat16
-I32 = mybir.dt.int32
 U32 = mybir.dt.uint32
 U8 = mybir.dt.uint8
 E5X4 = mybir.dt.float8_e5m2_x4
@@ -23,7 +22,6 @@ CH = GATES // NT
 EPS = 1e-5
 W_COPY = ("S", "S", "V", "S")
 XH_COPY = ("S", "S")
-HALF = GATES // 2
 
 
 def tile_layernormgrucell_pa_kernel(tc, x, h, W_irz, b_irz, W_hrz, b_hrz, out):
@@ -45,10 +43,6 @@ def tile_layernormgrucell_pa_kernel(tc, x, h, W_irz, b_irz, W_hrz, b_hrz, out):
         nc.scalar.activation(out=warm2[:], in_=warm[:], func=ACT.Sigmoid)
         ident = const.tile([P, P], F32, name="ident")
         make_identity(nc, ident[:])
-        brow = const.tile([P, 2 * GATES], BF16, name="brow")
-        nc.vector.memset(brow[:].bitcast(I32), 0)
-        ones = const.tile([P, P], BF16, name="ones")
-        nc.vector.memset(ones[:], 1.0)
         sums = const.tile([P, RT * 2 * CH], F32, name="sums")
         tot = const.tile([P, RT * 2], F32, name="tot")
         qq = const.tile([P, RT * 2], F32, name="qq")
@@ -77,13 +71,11 @@ def tile_layernormgrucell_pa_kernel(tc, x, h, W_irz, b_irz, W_hrz, b_hrz, out):
 
         load_a(0, 0)
         load_a(1, 0)
-        load_w(0, 0)
-        nc.sync.dma_start(out=brow[0:1, 0:GATES], in_=b_irz.rearrange("(o n) -> o n", o=1))
-        nc.sync.dma_start(out=brow[0:1, GATES : 2 * GATES], in_=b_hrz.rearrange("(o n) -> o n", o=1))
-        for c in range(1, CH):
-            load_w(0, c)
-        for c in range(CH):
-            load_w(1, c)
+        for s in range(2):
+            for c in range(CH):
+                load_w(s, c)
+        nc.sync.dma_start(out=bias[:, 0:GATES], in_=b_irz.partition_broadcast(P))
+        nc.sync.dma_start(out=bias[:, GATES : 2 * GATES], in_=b_hrz.partition_broadcast(P))
         for m in range(1, RT):
             load_a(0, m)
             load_a(1, m)
@@ -153,15 +145,6 @@ def tile_layernormgrucell_pa_kernel(tc, x, h, W_irz, b_irz, W_hrz, b_hrz, out):
             )
             ca[m] = codes
             sa[m] = scales
-
-        def spread_bias(jb):
-            pb = psum.tile([P, NT], F32, name="pb", tag="bank")
-            cols = slice(jb * NT, (jb + 1) * NT)
-            nc.tensor.matmul(out=pb[:], lhsT=ones[:], rhs=brow[:, cols], start=True, stop=True)
-            if jb % 2 == 0:
-                nc.vector.tensor_copy(out=bias[:, cols], in_=pb[:])
-            else:
-                nc.scalar.copy(out=bias[:, cols], in_=pb[:])
 
         accs = {}
         ys = {}
@@ -238,27 +221,27 @@ def tile_layernormgrucell_pa_kernel(tc, x, h, W_irz, b_irz, W_hrz, b_hrz, out):
             )
             fac[m] = (rr, rho, cc)
 
-        def combine(m, hf):
+        def combine(m, c0, c1):
             y1 = ys[(m, 0)]
             y2 = ys[(m, 1)]
             rho = fac[m][1]
-            cols = slice(hf * HALF, (hf + 1) * HALF)
+            cols = slice(c0 * NT, c1 * NT)
             nc.vector.scalar_tensor_tensor(
                 out=y1[:, cols], in0=y2[:, cols], scalar=rho[:, 0:1], in1=y1[:, cols], op0=ALU.mult, op1=ALU.add
             )
 
-        def squash(m):
+        def squash(m, c0, c1):
             y1 = ys[(m, 0)]
             rr = fac[m][0]
             cc = fac[m][2]
-            for hf in range(2):
-                cols = slice(hf * HALF, (hf + 1) * HALF)
-                nc.scalar.activation(
-                    out=y1[:, cols], in_=y1[:, cols], func=ACT.Sigmoid, bias=cc[:, 0:1], scale=rr[:, 0:1]
-                )
-                nc.sync.dma_start(out=out[m * P : (m + 1) * P, cols], in_=y1[:, cols])
+            cols = slice(c0 * NT, c1 * NT)
+            nc.scalar.activation(
+                out=y1[:, cols], in_=y1[:, cols], func=ACT.Sigmoid, bias=cc[:, 0:1], scale=rr[:, 0:1]
+            )
+            nc.sync.dma_start(out=out[m * P : (m + 1) * P, cols], in_=y1[:, cols])
 
         chunks = [(s, c) for s in range(2) for c in range(CH)]
+        LAST = RT - 1
         turn_a(0)
         for q in range(2 * CH):
             turn_w(chunks[q][0], chunks[q][1])
@@ -266,35 +249,45 @@ def tile_layernormgrucell_pa_kernel(tc, x, h, W_irz, b_irz, W_hrz, b_hrz, out):
                 quant_a(0)
             else:
                 quant_w(chunks[q - 1][0], chunks[q - 1][1])
-            if 2 <= q < 6:
-                spread_bias(2 * (q - 2))
-                spread_bias(2 * (q - 2) + 1)
-        turn_a(1)
         multiply(0, 0)
+        turn_a(1)
+        empty(0, 0)
         quant_w(1, CH - 1)
-        for i in range(RT + 2):
+        row_sum(0, 0)
+        square(0, 0)
+        for i in range(RT):
             if i >= 2:
-                squash(i - 2)
-            if 1 <= i <= RT:
+                squash(i - 2, 0, 2)
+                squash(i - 2, 2, 4)
+            if i >= 1:
                 factors(i - 1)
-            if i < RT:
                 empty(i, 0)
-                if i + 1 < RT:
-                    quant_a(i + 1)
+            if i < LAST:
+                quant_a(i + 1)
+            if i >= 1:
                 row_sum(i, 0)
                 square(i, 0)
-                multiply(i, 1)
-                if i + 2 < RT:
-                    turn_a(i + 2)
-                empty(i, 1)
-                if i >= 1:
-                    combine(i - 1, 0)
+            multiply(i, 1)
+            if i + 2 < RT:
+                turn_a(i + 2)
+            empty(i, 1)
+            if i == LAST:
                 row_sum(i, 1)
                 square(i, 1)
-                if i + 1 < RT:
-                    multiply(i + 1, 0)
+                combine(i - 1, 0, 2)
+                combine(i - 1, 2, 4)
+            else:
                 if i >= 1:
-                    combine(i - 1, 1)
-            if i == RT:
-                combine(i - 1, 0)
-                combine(i - 1, 1)
+                    combine(i - 1, 0, 2)
+                row_sum(i, 1)
+                square(i, 1)
+                multiply(i + 1, 0)
+                if i >= 1:
+                    combine(i - 1, 2, 4)
+        squash(LAST - 1, 0, 2)
+        squash(LAST - 1, 2, 4)
+        factors(LAST)
+        for c in range(CH):
+            combine(LAST, c, c + 1)
+        for c in range(CH):
+            squash(LAST, c, c + 1)

@@ -28,7 +28,7 @@ def tile_layernormgrucell_pa_kernel(tc, x, h, W_irz, b_irz, W_hrz, b_hrz, out):
     nc = tc.nc
     with ExitStack() as ctx:
         const = ctx.enter_context(tc.tile_pool(name="const", bufs=1))
-        wraw = ctx.enter_context(tc.tile_pool(name="wraw", bufs=8))
+        wraw = ctx.enter_context(tc.tile_pool(name="wraw", bufs=4))
         grp = ctx.enter_context(tc.tile_pool(name="grp", bufs=3))
         keep = ctx.enter_context(tc.tile_pool(name="keep", bufs=1))
         acts = ctx.enter_context(tc.tile_pool(name="acts", bufs=3))
@@ -56,13 +56,11 @@ def tile_layernormgrucell_pa_kernel(tc, x, h, W_irz, b_irz, W_hrz, b_hrz, out):
         ar = {}
 
         def load_w(s, c):
-            for hf in range(2):
-                t = wraw.tile([P, 2, K], BF16, name="wr", tag="wr")
-                r0 = c * NT + hf * 2 * P
-                nc.sync.dma_start(
-                    out=t[:], in_=weights[s][r0 : r0 + 2 * P, :].rearrange("(j p) k -> p j k", p=P)
-                )
-                wr[(s, c, hf)] = t
+            t = wraw.tile([P, 4, K], BF16, name="wr", tag="wr")
+            nc.sync.dma_start(
+                out=t[:], in_=weights[s][c * NT : (c + 1) * NT, :].rearrange("(p j) k -> p j k", j=4)
+            )
+            wr[(s, c)] = t
 
         def load_a(s, m):
             t = const.tile([P, K], BF16, name="ar%d_%d" % (s, m))
@@ -107,7 +105,7 @@ def tile_layernormgrucell_pa_kernel(tc, x, h, W_irz, b_irz, W_hrz, b_hrz, out):
         def turn_w(s, c):
             grouped = grp.tile([P, PASSES, NT, 4], BF16, name="gw", tag="gw", align_bytes=64)
             gwords = grouped[:].bitcast(F32)
-            banks = [transpose_rows(wr[(s, c, j // 2)][:, j % 2, :]) for j in range(4)]
+            banks = [transpose_rows(wr[(s, c)][:, j, :]) for j in range(4)]
             for j in range(4):
                 copy_out(W_COPY[j], gwords[:, :, j * P : (j + 1) * P, :], banks[j])
             gw[(s, c)] = grouped
@@ -170,10 +168,10 @@ def tile_layernormgrucell_pa_kernel(tc, x, h, W_irz, b_irz, W_hrz, b_hrz, out):
             i = m * 2 + s
             for c in range(CH):
                 nc.vector.scalar_tensor_tensor(
-                    out=y[:, c * NT : (c + 1) * NT],
-                    in0=accs[(m, s, c)][:],
+                    out=y[:, c * NT : (c + 1) * NT].rearrange("q (p j) -> q p j", j=4),
+                    in0=accs[(m, s, c)][:].rearrange("q (j p) -> q p j", j=4),
                     scalar=1.0,
-                    in1=bias[:, s * GATES + c * NT : s * GATES + (c + 1) * NT],
+                    in1=bias[:, s * GATES + c * NT : s * GATES + (c + 1) * NT].rearrange("q (p j) -> q p j", j=4),
                     op0=ALU.mult,
                     op1=ALU.add,
                     accum_out=sums[:, i * CH + c : i * CH + c + 1],

@@ -20,7 +20,7 @@ PASSES = K // (4 * P)
 RT = ROWS // P
 CH = GATES // NT
 EPS = 1e-5
-W_COPY = ("S", "S", "V", "S")
+W_COPY = ("S", "S", "S", "S")
 XH_COPY = ("S", "S")
 
 
@@ -28,7 +28,8 @@ def tile_layernormgrucell_pa_kernel(tc, x, h, W_irz, b_irz, W_hrz, b_hrz, out):
     nc = tc.nc
     with ExitStack() as ctx:
         const = ctx.enter_context(tc.tile_pool(name="const", bufs=1))
-        wraw = ctx.enter_context(tc.tile_pool(name="wraw", bufs=4))
+        wraw = ctx.enter_context(tc.tile_pool(name="wraw", bufs=3))
+        sorted_w = ctx.enter_context(tc.tile_pool(name="sorted_w", bufs=2))
         grp = ctx.enter_context(tc.tile_pool(name="grp", bufs=3))
         keep = ctx.enter_context(tc.tile_pool(name="keep", bufs=1))
         acts = ctx.enter_context(tc.tile_pool(name="acts", bufs=3))
@@ -91,6 +92,26 @@ def tile_layernormgrucell_pa_kernel(tc, x, h, W_irz, b_irz, W_hrz, b_hrz, out):
                     )
             return bank
 
+        def transpose_sorted(dw, j):
+            bank = psum.tile([P, NT], F32, name="tbank", tag="bank")
+            for g in range(PASSES):
+                for u in range(2):
+                    q = 2 * g + u
+                    nc.tensor.transpose(bank[:, q * P : (q + 1) * P], dw[:, j * PASSES + g, u, :], ident[:])
+            return bank
+
+        dws = {}
+
+        def sort_w(s, c):
+            dw = sorted_w.tile([P, 4 * PASSES, 2, P], F32, name="dw", tag="dw")
+            words = wr[(s, c)][:].rearrange("p j k -> p (j k)").bitcast(F32)
+            for hf in range(2):
+                nc.vector.tensor_copy(
+                    out=dw[:, hf * 4 : (hf + 1) * 4, :, :],
+                    in_=words[:, hf * 1024 : (hf + 1) * 1024].rearrange("p (a q u) -> p a u q", a=4, u=2),
+                )
+            dws[(s, c)] = dw
+
         def copy_out(eng, dst_words, bank):
             src = bank[:].rearrange("p (g u r) -> p g r u", g=PASSES, u=2)
             if eng == "S":
@@ -105,7 +126,7 @@ def tile_layernormgrucell_pa_kernel(tc, x, h, W_irz, b_irz, W_hrz, b_hrz, out):
         def turn_w(s, c):
             grouped = grp.tile([P, PASSES, NT, 4], BF16, name="gw", tag="gw", align_bytes=64)
             gwords = grouped[:].bitcast(F32)
-            banks = [transpose_rows(wr[(s, c)][:, j, :]) for j in range(4)]
+            banks = [transpose_sorted(dws[(s, c)], j) for j in range(4)]
             for j in range(4):
                 copy_out(W_COPY[j], gwords[:, :, j * P : (j + 1) * P, :], banks[j])
             gw[(s, c)] = grouped
@@ -240,9 +261,12 @@ def tile_layernormgrucell_pa_kernel(tc, x, h, W_irz, b_irz, W_hrz, b_hrz, out):
 
         chunks = [(s, c) for s in range(2) for c in range(CH)]
         LAST = RT - 1
+        sort_w(0, 0)
         turn_a(0)
         for q in range(2 * CH):
             turn_w(chunks[q][0], chunks[q][1])
+            if q + 1 < 2 * CH:
+                sort_w(chunks[q + 1][0], chunks[q + 1][1])
             if q == 0:
                 quant_a(0)
             else:

@@ -19,7 +19,9 @@ NT = 512
 PASSES = K // (4 * P)
 RT = ROWS // P
 CH = GATES // NT
+HALF = GATES // 2
 EPS = 1e-5
+PIECES = (0, 256, 768, 1280, 1792, 2048)
 W_COPY = ("S", "S", "S", "S")
 XH_COPY = ("S", "S")
 
@@ -74,8 +76,10 @@ def tile_layernormgrucell_pa_kernel(tc, x, h, W_irz, b_irz, W_hrz, b_hrz, out):
             for c in range(CH):
                 load_w(s, c)
         nc.sync.dma_start(out=bias[:, 0:GATES], in_=b_irz.partition_broadcast(P))
+        load_a(0, 1)
+        load_a(1, 1)
         nc.sync.dma_start(out=bias[:, GATES : 2 * GATES], in_=b_hrz.partition_broadcast(P))
-        for m in range(1, RT):
+        for m in range(2, RT):
             load_a(0, m)
             load_a(1, m)
 
@@ -240,11 +244,31 @@ def tile_layernormgrucell_pa_kernel(tc, x, h, W_irz, b_irz, W_hrz, b_hrz, out):
             )
             fac[m] = (rr, rho, cc)
 
+        def last_factors(m):
+            i = m * 2
+            vv = small.tile([P, 2], F32, name="vv", tag="vv")
+            nc.vector.tensor_scalar(
+                out=vv[:], in0=qq[:, i : i + 2], scalar1=2.0 ** -33, scalar2=EPS, op0=ALU.mult, op1=ALU.add
+            )
+            rr = small.tile([P, 2], F32, name="rr", tag="rr")
+            nc.gpsimd.tensor_tensor(out=rr[:], in0=vv[:], in1=neghalf[:], op=ALU.pow)
+            rho = small.tile([P, 1], F32, name="rho", tag="rho")
+            nc.vector.tensor_scalar(
+                out=rho[:], in0=vv[:, 0:1], scalar1=rr[:, 0:1], scalar2=rr[:, 1:2], op0=ALU.mult, op1=ALU.mult
+            )
+            mm = small.tile([P, 2], F32, name="mm", bufs=1)
+            nc.gpsimd.tensor_tensor(out=mm[:], in0=tot[:, i : i + 2], in1=rr[:], op=ALU.mult)
+            cc = small.tile([P, 1], F32, name="cc", tag="cc")
+            nc.gpsimd.tensor_scalar(
+                out=cc[:], in0=mm[:, 0:1], scalar1=mm[:, 1:2], scalar2=-(2.0 ** -11), op0=ALU.add, op1=ALU.mult
+            )
+            fac[m] = (rr, rho, cc)
+
         def combine(m, c0, c1):
             y1 = ys[(m, 0)]
             y2 = ys[(m, 1)]
             rho = fac[m][1]
-            cols = slice(c0 * NT, c1 * NT)
+            cols = slice(c0, c1)
             nc.vector.scalar_tensor_tensor(
                 out=y1[:, cols], in0=y2[:, cols], scalar=rho[:, 0:1], in1=y1[:, cols], op0=ALU.mult, op1=ALU.add
             )
@@ -253,7 +277,7 @@ def tile_layernormgrucell_pa_kernel(tc, x, h, W_irz, b_irz, W_hrz, b_hrz, out):
             y1 = ys[(m, 0)]
             rr = fac[m][0]
             cc = fac[m][2]
-            cols = slice(c0 * NT, c1 * NT)
+            cols = slice(c0, c1)
             nc.scalar.activation(
                 out=y1[:, cols], in_=y1[:, cols], func=ACT.Sigmoid, bias=cc[:, 0:1], scale=rr[:, 0:1]
             )
@@ -279,8 +303,8 @@ def tile_layernormgrucell_pa_kernel(tc, x, h, W_irz, b_irz, W_hrz, b_hrz, out):
         square(0, 0)
         for i in range(RT):
             if i >= 2:
-                squash(i - 2, 0, 2)
-                squash(i - 2, 2, 4)
+                squash(i - 2, 0, HALF)
+                squash(i - 2, HALF, GATES)
             if i >= 1:
                 factors(i - 1)
                 empty(i, 0)
@@ -296,20 +320,20 @@ def tile_layernormgrucell_pa_kernel(tc, x, h, W_irz, b_irz, W_hrz, b_hrz, out):
             if i == LAST:
                 row_sum(i, 1)
                 square(i, 1)
-                combine(i - 1, 0, 2)
-                combine(i - 1, 2, 4)
+                combine(i - 1, 0, HALF)
+                combine(i - 1, HALF, GATES)
             else:
                 if i >= 1:
-                    combine(i - 1, 0, 2)
+                    combine(i - 1, 0, HALF)
                 row_sum(i, 1)
                 square(i, 1)
                 multiply(i + 1, 0)
                 if i >= 1:
-                    combine(i - 1, 2, 4)
-        squash(LAST - 1, 0, 2)
-        squash(LAST - 1, 2, 4)
-        factors(LAST)
-        for c in range(CH):
-            combine(LAST, c, c + 1)
-        for c in range(CH):
-            squash(LAST, c, c + 1)
+                    combine(i - 1, HALF, GATES)
+        squash(LAST - 1, 0, HALF)
+        squash(LAST - 1, HALF, GATES)
+        last_factors(LAST)
+        for c0, c1 in zip(PIECES, PIECES[1:]):
+            combine(LAST, c0, c1)
+        for c0, c1 in zip(PIECES, PIECES[1:]):
+            squash(LAST, c0, c1)

from contextlib import ExitStack

import concourse.mybir as mybir
from concourse.masks import make_identity

F32 = mybir.dt.float32
BF16 = mybir.dt.bfloat16
U32 = mybir.dt.uint32
U8 = mybir.dt.uint8
E5X4 = mybir.dt.float8_e5m2_x4
ALU = mybir.AluOpType
ACT = mybir.ActivationFunctionType

ROWS, K, GATES = 1024, 1024, 2048
FLOPS = 2 * 2 * ROWS * K * GATES

P = 128
NT = 512
PASSES = K // (4 * P)
RT = ROWS // P
CH = GATES // NT
HALF = GATES // 2
EPS = 1e-5
PIECES = (0, 256, 768, 1280, 1792, 2048)
W_COPY = ("S", "S", "S", "S")
XH_COPY = ("S", "S")


def tile_layernormgrucell_pa_kernel(tc, x, h, W_irz, b_irz, W_hrz, b_hrz, out):
    nc = tc.nc
    with ExitStack() as ctx:
        const = ctx.enter_context(tc.tile_pool(name="const", bufs=1))
        wraw = ctx.enter_context(tc.tile_pool(name="wraw", bufs=3))
        sorted_w = ctx.enter_context(tc.tile_pool(name="sorted_w", bufs=2))
        grp = ctx.enter_context(tc.tile_pool(name="grp", bufs=3))
        keep = ctx.enter_context(tc.tile_pool(name="keep", bufs=1))
        acts = ctx.enter_context(tc.tile_pool(name="acts", bufs=3))
        ypool = ctx.enter_context(tc.tile_pool(name="ypool", bufs=3))
        small = ctx.enter_context(tc.tile_pool(name="small", bufs=3))
        psum = ctx.enter_context(tc.psum_pool(name="psum", bufs=8))
        ctx.enter_context(tc.manual_schedule())

        warm = const.tile([P, 1], F32, name="warm")
        nc.vector.memset(warm[:], 0.0)
        warm2 = const.tile([P, 1], F32, name="warm2")
        nc.scalar.activation(out=warm2[:], in_=warm[:], func=ACT.Sigmoid)
        ident = const.tile([P, P], F32, name="ident")
        make_identity(nc, ident[:])
        sums = const.tile([P, RT * 2 * CH], F32, name="sums")
        tot = const.tile([P, RT * 2], F32, name="tot")
        qq = const.tile([P, RT * 2], F32, name="qq")
        neghalf = const.tile([P, 2], F32, name="neghalf")
        nc.vector.memset(neghalf[:], -0.5)
        bias = const.tile([P, 2 * GATES], BF16, name="bias")

        weights = (W_irz, W_hrz)
        rows_in = (x, h)
        wr = {}
        ar = {}

        def load_w(s, c):
            t = wraw.tile([P, 4, K], BF16, name="wr", tag="wr")
            nc.sync.dma_start(
                out=t[:], in_=weights[s][c * NT : (c + 1) * NT, :].rearrange("(p j) k -> p j k", j=4)
            )
            wr[(s, c)] = t

        def load_a(s, m):
            t = const.tile([P, K], BF16, name="ar%d_%d" % (s, m))
            nc.sync.dma_start(out=t[:], in_=rows_in[s][m * P : (m + 1) * P, :])
            ar[(s, m)] = t

        load_a(0, 0)
        load_a(1, 0)
        for s in range(2):
            for c in range(CH):
                load_w(s, c)
        nc.sync.dma_start(out=bias[:, 0:GATES], in_=b_irz.partition_broadcast(P))
        load_a(0, 1)
        load_a(1, 1)
        nc.sync.dma_start(out=bias[:, GATES : 2 * GATES], in_=b_hrz.partition_broadcast(P))
        for m in range(2, RT):
            load_a(0, m)
            load_a(1, m)

        def transpose_rows(raw2d):
            words = raw2d.bitcast(F32)
            bank = psum.tile([P, NT], F32, name="tbank", tag="bank")
            for g in range(PASSES):
                for u in range(2):
                    q = 2 * g + u
                    nc.tensor.transpose(
                        bank[:, q * P : (q + 1) * P],
                        words[:, 256 * g + u : 256 * (g + 1) : 2],
                        ident[:],
                    )
            return bank

        def transpose_sorted(dw, j):
            bank = psum.tile([P, NT], F32, name="tbank", tag="bank")
            for g in range(PASSES):
                for u in range(2):
                    q = 2 * g + u
                    nc.tensor.transpose(bank[:, q * P : (q + 1) * P], dw[:, j * PASSES + g, u, :], ident[:])
            return bank

        dws = {}

        def sort_w(s, c):
            dw = sorted_w.tile([P, 4 * PASSES, 2, P], F32, name="dw", tag="dw")
            words = wr[(s, c)][:].rearrange("p j k -> p (j k)").bitcast(F32)
            for hf in range(2):
                nc.vector.tensor_copy(
                    out=dw[:, hf * 4 : (hf + 1) * 4, :, :],
                    in_=words[:, hf * 1024 : (hf + 1) * 1024].rearrange("p (a q u) -> p a u q", a=4, u=2),
                )
            dws[(s, c)] = dw

        def copy_out(eng, dst_words, bank):
            src = bank[:].rearrange("p (g u r) -> p g r u", g=PASSES, u=2)
            if eng == "S":
                nc.scalar.copy(out=dst_words, in_=src)
            else:
                nc.vector.tensor_copy(out=dst_words, in_=src)

        gw = {}
        cw = {}
        sw = {}

        def turn_w(s, c):
            grouped = grp.tile([P, PASSES, NT, 4], BF16, name="gw", tag="gw", align_bytes=64)
            gwords = grouped[:].bitcast(F32)
            banks = [transpose_sorted(dws[(s, c)], j) for j in range(4)]
            for j in range(4):
                copy_out(W_COPY[j], gwords[:, :, j * P : (j + 1) * P, :], banks[j])
            gw[(s, c)] = grouped

        def quant_w(s, c):
            codes = keep.tile([P, PASSES, NT], U32, name="cw%d_%d" % (s, c), align_bytes=64)
            scales = keep.tile([P, PASSES, NT], U8, name="sw%d_%d" % (s, c), align_bytes=64)
            nc.vector.quantize_mx(
                out=codes[:].rearrange("p g n -> p (g n)").bitcast(E5X4),
                scales=scales[:].rearrange("p g n -> p (g n)"),
                in_=gw[(s, c)][:].rearrange("p g n t -> p (g n t)"),
            )
            cw[(s, c)] = codes
            sw[(s, c)] = scales

        ga = {}
        ca = {}
        sa = {}

        def turn_a(m):
            grouped = grp.tile([P, 2, PASSES, P, 4], BF16, name="ga", tag="ga", align_bytes=64)
            gwords = grouped[:].bitcast(F32)
            banks = [transpose_rows(ar[(s, m)][:]) for s in range(2)]
            for s in range(2):
                copy_out(XH_COPY[s], gwords[:, s, :, :, :], banks[s])
            ga[m] = grouped

        def quant_a(m):
            codes = acts.tile([P, 2, PASSES, P], U32, name="ca", tag="ca", align_bytes=64)
            scales = acts.tile([P, 2, PASSES, P], U8, name="sa", tag="sa", align_bytes=64)
            nc.vector.quantize_mx(
                out=codes[:].rearrange("p s g n -> p (s g n)").bitcast(E5X4),
                scales=scales[:].rearrange("p s g n -> p (s g n)"),
                in_=ga[m][:].rearrange("p s g n t -> p (s g n t)"),
            )
            ca[m] = codes
            sa[m] = scales

        accs = {}
        ys = {}

        def multiply(m, s):
            for c in range(CH):
                acc = psum.tile([P, NT], F32, name="acc", tag="bank")
                for g in range(PASSES):
                    nc.tensor.matmul_mx(
                        out=acc[:],
                        lhsT=ca[m][:, s, g, :].bitcast(E5X4),
                        lhsT_scale=sa[m][:, s, g, :],
                        rhs=cw[(s, c)][:, g, :].bitcast(E5X4),
                        rhs_scale=sw[(s, c)][:, g, :],
                        start=(g == 0),
                        stop=(g == PASSES - 1),
                    )
                accs[(m, s, c)] = acc

        def empty(m, s):
            y = ypool.tile([P, GATES], F32, name="y%d" % s, tag="y%d" % s)
            ys[(m, s)] = y
            i = m * 2 + s
            for c in range(CH):
                nc.vector.scalar_tensor_tensor(
                    out=y[:, c * NT : (c + 1) * NT].rearrange("q (p j) -> q p j", j=4),
                    in0=accs[(m, s, c)][:].rearrange("q (j p) -> q p j", j=4),
                    scalar=1.0,
                    in1=bias[:, s * GATES + c * NT : s * GATES + (c + 1) * NT].rearrange("q (p j) -> q p j", j=4),
                    op0=ALU.mult,
                    op1=ALU.add,
                    accum_out=sums[:, i * CH + c : i * CH + c + 1],
                )

        def row_sum(m, s):
            i = m * 2 + s
            nc.vector.tensor_reduce(
                out=tot[:, i : i + 1], in_=sums[:, i * CH : (i + 1) * CH], axis=mybir.AxisListType.X, op=ALU.add
            )

        def square(m, s):
            i = m * 2 + s
            junk = small.tile([P, GATES], BF16, name="junk", tag="junk", bufs=2)
            nc.scalar.activation(
                out=junk[:],
                in_=ys[(m, s)][:],
                func=ACT.Square,
                bias=tot[:, i : i + 1],
                scale=-2048.0,
                accum_out=qq[:, i : i + 1],
            )

        fac = {}

        def factors(m):
            i = m * 2
            vv = small.tile([P, 2], F32, name="vv", tag="vv")
            nc.gpsimd.tensor_scalar(
                out=vv[:], in0=qq[:, i : i + 2], scalar1=2.0 ** -33, scalar2=EPS, op0=ALU.mult, op1=ALU.add
            )
            rr = small.tile([P, 2], F32, name="rr", tag="rr")
            nc.gpsimd.tensor_tensor(out=rr[:], in0=vv[:], in1=neghalf[:], op=ALU.pow)
            rho = small.tile([P, 1], F32, name="rho", tag="rho")
            nc.gpsimd.tensor_scalar(
                out=rho[:], in0=vv[:, 0:1], scalar1=rr[:, 0:1], scalar2=rr[:, 1:2], op0=ALU.mult, op1=ALU.mult
            )
            kp = small.tile([P, 1], F32, name="kp", tag="kp")
            nc.gpsimd.tensor_scalar(
                out=kp[:], in0=tot[:, i + 1 : i + 2], scalar1=rho[:, 0:1], scalar2=tot[:, i : i + 1], op0=ALU.mult, op1=ALU.add
            )
            cc = small.tile([P, 1], F32, name="cc", tag="cc")
            nc.gpsimd.tensor_scalar(
                out=cc[:], in0=kp[:], scalar1=rr[:, 0:1], scalar2=-(2.0 ** -11), op0=ALU.mult, op1=ALU.mult
            )
            fac[m] = (rr, rho, cc)

        def last_factors(m):
            i = m * 2
            vv = small.tile([P, 2], F32, name="vv", tag="vv")
            nc.vector.tensor_scalar(
                out=vv[:], in0=qq[:, i : i + 2], scalar1=2.0 ** -33, scalar2=EPS, op0=ALU.mult, op1=ALU.add
            )
            rr = small.tile([P, 2], F32, name="rr", tag="rr")
            nc.gpsimd.tensor_tensor(out=rr[:], in0=vv[:], in1=neghalf[:], op=ALU.pow)
            rho = small.tile([P, 1], F32, name="rho", tag="rho")
            nc.vector.tensor_scalar(
                out=rho[:], in0=vv[:, 0:1], scalar1=rr[:, 0:1], scalar2=rr[:, 1:2], op0=ALU.mult, op1=ALU.mult
            )
            mm = small.tile([P, 2], F32, name="mm", bufs=1)
            nc.gpsimd.tensor_tensor(out=mm[:], in0=tot[:, i : i + 2], in1=rr[:], op=ALU.mult)
            cc = small.tile([P, 1], F32, name="cc", tag="cc")
            nc.gpsimd.tensor_scalar(
                out=cc[:], in0=mm[:, 0:1], scalar1=mm[:, 1:2], scalar2=-(2.0 ** -11), op0=ALU.add, op1=ALU.mult
            )
            fac[m] = (rr, rho, cc)

        def combine(m, c0, c1):
            y1 = ys[(m, 0)]
            y2 = ys[(m, 1)]
            rho = fac[m][1]
            cols = slice(c0, c1)
            nc.vector.scalar_tensor_tensor(
                out=y1[:, cols], in0=y2[:, cols], scalar=rho[:, 0:1], in1=y1[:, cols], op0=ALU.mult, op1=ALU.add
            )

        def squash(m, c0, c1):
            y1 = ys[(m, 0)]
            rr = fac[m][0]
            cc = fac[m][2]
            cols = slice(c0, c1)
            nc.scalar.activation(
                out=y1[:, cols], in_=y1[:, cols], func=ACT.Sigmoid, bias=cc[:, 0:1], scale=rr[:, 0:1]
            )
            nc.sync.dma_start(out=out[m * P : (m + 1) * P, cols], in_=y1[:, cols])

        chunks = [(s, c) for s in range(2) for c in range(CH)]
        LAST = RT - 1
        sort_w(0, 0)
        turn_a(0)
        for q in range(2 * CH):
            turn_w(chunks[q][0], chunks[q][1])
            if q + 1 < 2 * CH:
                sort_w(chunks[q + 1][0], chunks[q + 1][1])
            if q == 0:
                quant_a(0)
            else:
                quant_w(chunks[q - 1][0], chunks[q - 1][1])
        multiply(0, 0)
        turn_a(1)
        empty(0, 0)
        quant_w(1, CH - 1)
        row_sum(0, 0)
        square(0, 0)
        for i in range(RT):
            if i >= 2:
                squash(i - 2, 0, HALF)
                squash(i - 2, HALF, GATES)
            if i >= 1:
                factors(i - 1)
                empty(i, 0)
            if i < LAST:
                quant_a(i + 1)
            if i >= 1:
                row_sum(i, 0)
                square(i, 0)
            multiply(i, 1)
            if i + 2 < RT:
                turn_a(i + 2)
            empty(i, 1)
            if i == LAST:
                row_sum(i, 1)
                square(i, 1)
                combine(i - 1, 0, HALF)
                combine(i - 1, HALF, GATES)
            else:
                if i >= 1:
                    combine(i - 1, 0, HALF)
                row_sum(i, 1)
                square(i, 1)
                multiply(i + 1, 0)
                if i >= 1:
                    combine(i - 1, HALF, GATES)
        squash(LAST - 1, 0, HALF)
        squash(LAST - 1, HALF, GATES)
        last_factors(LAST)
        for c0, c1 in zip(PIECES, PIECES[1:]):
            combine(LAST, c0, c1)
        for c0, c1 in zip(PIECES, PIECES[1:]):
            squash(LAST, c0, c1)
